import numpy as np
import ml_dtypes


def mxq(x, axis, fmt="e4m3"):
    dtype, down = {"e4m3": (ml_dtypes.float8_e4m3fn, 7), "e5m2": (ml_dtypes.float8_e5m2, 14)}[fmt]
    v = np.moveaxis(np.asarray(x, np.float32).astype(ml_dtypes.bfloat16).astype(np.float64), axis, -1)
    blocks = v.reshape(v.shape[:-1] + (-1, 32))
    amax = np.abs(blocks).max(-1, keepdims=True)
    byte = np.maximum(np.where(amax > 0, np.frexp(amax)[1] - 1 + 127, 0) - down, 1)
    scale = np.exp2(byte - 127.0)
    codes = (blocks / scale).astype(np.float32).astype(dtype).astype(np.float64)
    return np.moveaxis((codes * scale).reshape(v.shape), -1, axis)


WIDE = False


def mx_kscale(k):
    if not WIDE:
        return np.ones(k)
    levels = np.array([20, -20, 10, -10, 0])
    a = np.random.permutation(np.resize(levels, k // 512 * 4)).reshape(k // 512, 4)
    idx = np.arange(k)
    return np.exp2(a[idx // 512, idx % 128 // 32])


BF16 = ml_dtypes.bfloat16


def bf(x):
    return np.asarray(x, np.float32).astype(BF16)


def f64(x):
    return np.asarray(x).astype(np.float64)


B, T, C, H, NOPE, ROPE, VD, LORA = 1, 512, 512, 16, 32, 32, 128, 512
QK = NOPE + ROPE
HALF = ROPE // 2


def make_freq_cis():
    inv = 1.0 / (10000.0 ** (np.arange(0, ROPE, 2) / ROPE))
    ang = np.outer(np.arange(T), inv)
    return np.stack([np.cos(ang), np.sin(ang)], -1)


def apply_rope(v, fc):
    vr = v.reshape(B, T, H, HALF, 2)
    f = fc.reshape(1, T, 1, HALF, 2)
    real = vr[..., 0] * f[..., 0] - vr[..., 1] * f[..., 1]
    imag = vr[..., 1] * f[..., 0] + vr[..., 0] * f[..., 1]
    return np.stack([real, imag], -1).reshape(B, T, H, ROPE)


def apply_rope_adjoint(g, fc):
    gr = g.reshape(B, T, H, HALF, 2)
    f = fc.reshape(1, T, 1, HALF, 2)
    a = gr[..., 0] * f[..., 0] + gr[..., 1] * f[..., 1]
    b = gr[..., 1] * f[..., 0] - gr[..., 0] * f[..., 1]
    return np.stack([a, b], -1).reshape(B, T, H, ROPE)


def setup_inputs():
    u = mx_kscale(H * QK)
    u = np.repeat(u[::2], 2)
    x = np.random.standard_normal((B, T, C))
    fc = make_freq_cis()
    Wq = np.random.standard_normal((C, H * QK)) * 2.0 / np.sqrt(C) / u[None, :]
    g = np.random.standard_normal((B, T, H, QK)) * np.exp2(np.random.randint(-12, 1, (B, T, 1, 1))) * 8.0 * u.reshape(H, QK)
    return {"x": bf(x), "freq_cis": bf(fc), "Wq": bf(Wq), "grad_out": bf(g)}


def reference(x, freq_cis, Wq, grad_out):
    g = f64(grad_out)
    gp = np.concatenate([g[..., :NOPE], apply_rope_adjoint(g[..., NOPE:], f64(freq_cis))], -1).reshape(B, T, H * QK)
    return mxq(gp, 2, "e5m2") @ mxq(f64(Wq), 1, "e4m3").T

@@ -1,0 +1,171 @@
+from contextlib import ExitStack
+
+import concourse.mybir as mybir
+from concourse.masks import make_identity
+
+BF16 = mybir.dt.bfloat16
+F32 = mybir.dt.float32
+U32 = mybir.dt.uint32
+U8 = mybir.dt.uint8
+E4M3_X4 = mybir.dt.float8_e4m3fn_x4
+E5M2_X4 = mybir.dt.float8_e5m2_x4
+MULT = mybir.AluOpType.mult
+ADD = mybir.AluOpType.add
+
+P = 128
+T = 512
+C = 512
+HEADS = 16
+HEAD_DIM = 64
+KEPT = 32
+PAIRS = 16
+K = HEADS * HEAD_DIM
+K_PASS = 4 * P
+PASSES = K // K_PASS
+T_TILES = T // P
+C_TILES = C // P
+WORDS = K // 2
+BLOCKS = WORDS // P
+
+FLOPS = 2 * T * C * K
+BYTES = 2 * (T * 2 * PAIRS + C * K + T * K) + 4 * T * C
+
+
+def turn_rows(nc, bank_pool, rows, identity, grouped_words):
+    bank = bank_pool.tile([P, BLOCKS, P], F32)
+    words = rows.bitcast(F32)
+    for j in range(BLOCKS):
+        nc.tensor.transpose(bank[:, j, :], words[:, j * P : (j + 1) * P], identity)
+    nc.scalar.copy(out=grouped_words, in_=bank.rearrange("p (g u) r -> p g r u", u=2))
+
+
+def tile_multiheadlatentattention_pb_s_kernel(tc, x, freq_cis, Wq, grad_out, out):
+    nc = tc.nc
+    g_dram = grad_out[0].rearrange("(p n) h f -> p n (h f)", n=T_TILES)
+    table_dram = freq_cis.rearrange("(p n) i c -> p n i c", n=T_TILES)
+    out_dram = out[0].rearrange("(p n) c -> p n c", n=T_TILES)
+
+    with ExitStack() as stack:
+        stack.enter_context(tc.manual_schedule())
+        keep = stack.enter_context(tc.tile_pool(name="keep", bufs=1))
+        g_pool = stack.enter_context(tc.tile_pool(name="g", bufs=T_TILES))
+        w_pool = stack.enter_context(tc.tile_pool(name="w", bufs=C_TILES))
+        product_pool = stack.enter_context(tc.tile_pool(name="products", bufs=2))
+        grouped_pool = stack.enter_context(tc.tile_pool(name="grouped", bufs=T_TILES))
+        result_pool = stack.enter_context(tc.tile_pool(name="result", bufs=T_TILES))
+        bank_pool = stack.enter_context(tc.psum_pool(name="turned", bufs=4))
+        acc_pool = stack.enter_context(tc.psum_pool(name="acc", bufs=T_TILES))
+
+        table = keep.tile([P, T_TILES, PAIRS, 2], BF16)
+        nc.sync.dma_start(out=table, in_=table_dram)
+        g_tiles = []
+        for n in range(T_TILES):
+            g_rows = g_pool.tile([P, K], BF16)
+            nc.sync.dma_start(out=g_rows, in_=g_dram[:, n, :])
+            g_tiles.append(g_rows)
+        w_tiles = []
+        for j in range(C_TILES):
+            w_rows = w_pool.tile([P, K], BF16)
+            nc.sync.dma_start(out=w_rows, in_=Wq[j * P : (j + 1) * P, :])
+            w_tiles.append(w_rows)
+
+        identity = keep.tile([P, P], F32)
+        make_identity(nc, identity)
+
+        minus_sin = keep.tile([P, T_TILES, PAIRS], BF16)
+        nc.vector.tensor_scalar_mul(out=minus_sin, in0=table[:, :, :, 1], scalar1=-1.0)
+
+        w_grouped = keep.tile([P, PASSES * C * 4], BF16, align_bytes=64)
+        w_grouped_words = w_grouped.bitcast(F32).rearrange("p (g c u) -> p g c u", g=PASSES, u=2)
+        for j in range(C_TILES):
+            turn_rows(nc, bank_pool, w_tiles[j], identity, w_grouped_words[:, :, j * P : (j + 1) * P, :])
+
+        def rotated_part(n):
+            by_head = g_tiles[n].rearrange("p (h f) -> p h f", f=HEAD_DIM)
+            return by_head[:, :, KEPT:HEAD_DIM].rearrange("p h (i q) -> p h i q", q=2)
+
+        def products(n):
+            e = rotated_part(n)
+            cos = table[:, n, :, 0]
+            sin = table[:, n, :, 1]
+            with_cos = product_pool.tile([P, HEADS, PAIRS, 2], F32)
+            with_sin = product_pool.tile([P, 2, HEADS, PAIRS], F32)
+            nc.vector.tensor_tensor(
+                out=with_cos,
+                in0=e,
+                in1=cos.unsqueeze(1).unsqueeze(3).to_broadcast([P, HEADS, PAIRS, 2]),
+                op=MULT,
+            )
+            nc.vector.tensor_tensor(
+                out=with_sin[:, 0],
+                in0=e[:, :, :, 1],
+                in1=sin.unsqueeze(1).to_broadcast([P, HEADS, PAIRS]),
+                op=MULT,
+            )
+            nc.vector.tensor_tensor(
+                out=with_sin[:, 1],
+                in0=e[:, :, :, 0],
+                in1=minus_sin[:, n, :].unsqueeze(1).to_broadcast([P, HEADS, PAIRS]),
+                op=MULT,
+            )
+            return with_cos, with_sin
+
+        gp_grouped = []
+
+        def add_and_turn(n, with_cos, with_sin):
+            nc.vector.tensor_tensor(
+                out=rotated_part(n),
+                in0=with_cos,
+                in1=with_sin.rearrange("p q h i -> p h i q"),
+                op=ADD,
+            )
+            grouped = grouped_pool.tile([P, PASSES * P * 4], BF16, align_bytes=64)
+            turn_rows(
+                nc,
+                bank_pool,
+                g_tiles[n],
+                identity,
+                grouped.bitcast(F32).rearrange("p (g r u) -> p g r u", g=PASSES, u=2),
+            )
+            gp_grouped.append(grouped)
+
+        waiting = products(0)
+        for n in range(1, T_TILES):
+            fresh = products(n)
+            add_and_turn(n - 1, *waiting)
+            waiting = fresh
+        add_and_turn(T_TILES - 1, *waiting)
+
+        w_codes = keep.tile([P, PASSES, C], U32, align_bytes=64)
+        w_scales = keep.tile([P, PASSES, C], U8, align_bytes=64)
+        for g in range(PASSES):
+            nc.vector.quantize_mx(
+                out=w_codes[:, g, :].bitcast(E4M3_X4),
+                scales=w_scales[:, g, :],
+                in_=w_grouped[:, g * C * 4 : (g + 1) * C * 4],
+            )
+        gp_codes = keep.tile([P, T_TILES, PASSES * P], U32, align_bytes=64)
+        gp_scales = keep.tile([P, T_TILES, PASSES * P], U8, align_bytes=64)
+        for n in range(T_TILES):
+            nc.vector.quantize_mx(
+                out=gp_codes[:, n, :].bitcast(E5M2_X4),
+                scales=gp_scales[:, n, :],
+                in_=gp_grouped[n],
+            )
+
+        for n in range(T_TILES):
+            acc = acc_pool.tile([P, C], F32)
+            for g in range(PASSES):
+                tokens = slice(g * P, (g + 1) * P)
+                nc.tensor.matmul_mx(
+                    out=acc,
+                    lhsT=gp_codes[:, n, tokens].bitcast(E5M2_X4),
+                    lhsT_scale=gp_scales[:, n, tokens],
+                    rhs=w_codes[:, g, :].bitcast(E4M3_X4),
+                    rhs_scale=w_scales[:, g, :],
+                    start=(g == 0),
+                    stop=(g == PASSES - 1),
+                )
+            result = result_pool.tile([P, C], F32)
+            nc.scalar.copy(out=result, in_=acc)
+            nc.sync.dma_start(out=out_dram[:, n, :], in_=result)

@@ -31,141 +31,189 @@ FLOPS = 2 * T * C * K
 BYTES = 2 * (T * 2 * PAIRS + C * K + T * K) + 4 * T * C
 
 
-def turn_rows(nc, bank_pool, rows, identity, grouped_words):
-    bank = bank_pool.tile([P, BLOCKS, P], F32)
-    words = rows.bitcast(F32)
-    for j in range(BLOCKS):
-        nc.tensor.transpose(bank[:, j, :], words[:, j * P : (j + 1) * P], identity)
-    nc.scalar.copy(out=grouped_words, in_=bank.rearrange("p (g u) r -> p g r u", u=2))
-
-
 def tile_multiheadlatentattention_pb_s_kernel(tc, x, freq_cis, Wq, grad_out, out):
     nc = tc.nc
     g_dram = grad_out[0].rearrange("(p n) h f -> p n (h f)", n=T_TILES)
     table_dram = freq_cis.rearrange("(p n) i c -> p n i c", n=T_TILES)
     out_dram = out[0].rearrange("(p n) c -> p n c", n=T_TILES)
+    ROT = 2 * PAIRS
 
     with ExitStack() as stack:
         stack.enter_context(tc.manual_schedule())
         keep = stack.enter_context(tc.tile_pool(name="keep", bufs=1))
         g_pool = stack.enter_context(tc.tile_pool(name="g", bufs=T_TILES))
         w_pool = stack.enter_context(tc.tile_pool(name="w", bufs=C_TILES))
-        product_pool = stack.enter_context(tc.tile_pool(name="products", bufs=2))
+        product_pool = stack.enter_context(tc.tile_pool(name="products", bufs=T_TILES))
         grouped_pool = stack.enter_context(tc.tile_pool(name="grouped", bufs=T_TILES))
         result_pool = stack.enter_context(tc.tile_pool(name="result", bufs=T_TILES))
-        bank_pool = stack.enter_context(tc.psum_pool(name="turned", bufs=4))
+        bank_pool = stack.enter_context(tc.psum_pool(name="turned", bufs=3))
+        coef_pool = stack.enter_context(tc.psum_pool(name="coefbank", bufs=1))
         acc_pool = stack.enter_context(tc.psum_pool(name="acc", bufs=T_TILES))
 
         table = keep.tile([P, T_TILES, PAIRS, 2], BF16)
         nc.sync.dma_start(out=table, in_=table_dram)
-        g_tiles = []
-        for n in range(T_TILES):
-            g_rows = g_pool.tile([P, K], BF16)
-            nc.sync.dma_start(out=g_rows, in_=g_dram[:, n, :])
-            g_tiles.append(g_rows)
-        w_tiles = []
-        for j in range(C_TILES):
-            w_rows = w_pool.tile([P, K], BF16)
-            nc.sync.dma_start(out=w_rows, in_=Wq[j * P : (j + 1) * P, :])
-            w_tiles.append(w_rows)
+        g_tiles = {}
+        w_tiles = {}
+        for kind, j in (("g", 0), ("w", 0), ("g", 1), ("w", 1), ("g", 2), ("w", 2), ("g", 3), ("w", 3)):
+            if kind == "g":
+                g_rows = g_pool.tile([P, K], BF16)
+                nc.sync.dma_start(out=g_rows, in_=g_dram[:, j, :])
+                g_tiles[j] = g_rows
+            else:
+                w_rows = w_pool.tile([P, K], BF16)
+                nc.sync.dma_start(out=w_rows, in_=Wq[j * P : (j + 1) * P, :])
+                w_tiles[j] = w_rows
 
         identity = keep.tile([P, P], F32)
         make_identity(nc, identity)
+        sign = keep.tile([P, 2], BF16)
+        nc.gpsimd.memset(sign, 1.0)
+        nc.gpsimd.memset(sign[:, 0:1], -1.0)
 
-        minus_sin = keep.tile([P, T_TILES, PAIRS], BF16)
-        nc.vector.tensor_scalar_mul(out=minus_sin, in0=table[:, :, :, 1], scalar1=-1.0)
+        identity_bf = keep.tile([P, P], BF16)
+        nc.vector.tensor_copy(out=identity_bf, in_=identity)
+        coef = keep.tile([P, T_TILES, 2, ROT], BF16)
+        shape4 = [P, T_TILES, PAIRS, 2]
+        nc.vector.tensor_copy(
+            out=coef[:, :, 0, :].rearrange("p n (i q) -> p n i q", q=2),
+            in_=table[:, :, :, 0].unsqueeze(3).to_broadcast(shape4),
+        )
+        nc.vector.tensor_tensor(
+            out=coef[:, :, 1, :].rearrange("p n (i q) -> p n i q", q=2),
+            in0=table[:, :, :, 1].unsqueeze(3).to_broadcast(shape4),
+            in1=sign.unsqueeze(1).unsqueeze(1).to_broadcast(shape4),
+            op=MULT,
+        )
+
+        coef_bank = coef_pool.tile([P, T_TILES, 2, ROT], F32)
+        nc.tensor.matmul(
+            coef_bank.rearrange("p n r f -> p (n r f)"),
+            lhsT=identity_bf,
+            rhs=coef.rearrange("p n r f -> p (n r f)"),
+            start=True,
+            stop=True,
+        )
 
         w_grouped = keep.tile([P, PASSES * C * 4], BF16, align_bytes=64)
         w_grouped_words = w_grouped.bitcast(F32).rearrange("p (g c u) -> p g c u", g=PASSES, u=2)
-        for j in range(C_TILES):
-            turn_rows(nc, bank_pool, w_tiles[j], identity, w_grouped_words[:, :, j * P : (j + 1) * P, :])
-
-        def rotated_part(n):
-            by_head = g_tiles[n].rearrange("p (h f) -> p h f", f=HEAD_DIM)
-            return by_head[:, :, KEPT:HEAD_DIM].rearrange("p h (i q) -> p h i q", q=2)
-
-        def products(n):
-            e = rotated_part(n)
-            cos = table[:, n, :, 0]
-            sin = table[:, n, :, 1]
-            with_cos = product_pool.tile([P, HEADS, PAIRS, 2], F32)
-            with_sin = product_pool.tile([P, 2, HEADS, PAIRS], F32)
-            nc.vector.tensor_tensor(
-                out=with_cos,
-                in0=e,
-                in1=cos.unsqueeze(1).unsqueeze(3).to_broadcast([P, HEADS, PAIRS, 2]),
-                op=MULT,
-            )
-            nc.vector.tensor_tensor(
-                out=with_sin[:, 0],
-                in0=e[:, :, :, 1],
-                in1=sin.unsqueeze(1).to_broadcast([P, HEADS, PAIRS]),
-                op=MULT,
-            )
-            nc.vector.tensor_tensor(
-                out=with_sin[:, 1],
-                in0=e[:, :, :, 0],
-                in1=minus_sin[:, n, :].unsqueeze(1).to_broadcast([P, HEADS, PAIRS]),
-                op=MULT,
-            )
-            return with_cos, with_sin
-
-        gp_grouped = []
-
-        def add_and_turn(n, with_cos, with_sin):
-            nc.vector.tensor_tensor(
-                out=rotated_part(n),
-                in0=with_cos,
-                in1=with_sin.rearrange("p q h i -> p h i q"),
-                op=ADD,
-            )
-            grouped = grouped_pool.tile([P, PASSES * P * 4], BF16, align_bytes=64)
-            turn_rows(
-                nc,
-                bank_pool,
-                g_tiles[n],
-                identity,
-                grouped.bitcast(F32).rearrange("p (g r u) -> p g r u", g=PASSES, u=2),
-            )
-            gp_grouped.append(grouped)
-
-        waiting = products(0)
-        for n in range(1, T_TILES):
-            fresh = products(n)
-            add_and_turn(n - 1, *waiting)
-            waiting = fresh
-        add_and_turn(T_TILES - 1, *waiting)
-
         w_codes = keep.tile([P, PASSES, C], U32, align_bytes=64)
         w_scales = keep.tile([P, PASSES, C], U8, align_bytes=64)
-        for g in range(PASSES):
+        gp_codes = keep.tile([P, T_TILES, PASSES * P], U32, align_bytes=64)
+        gp_scales = keep.tile([P, T_TILES, PASSES * P], U8, align_bytes=64)
+
+        def turn(rows, grouped_words):
+            bank = bank_pool.tile([P, BLOCKS, P], F32)
+            words = rows.bitcast(F32)
+            for j in range(BLOCKS):
+                nc.tensor.transpose(bank[:, j, :], words[:, j * P : (j + 1) * P], identity)
+            nc.scalar.copy(out=grouped_words, in_=bank.rearrange("p (g u) r -> p g r u", u=2))
+
+        def turn_w(j):
+            turn(w_tiles[j], w_grouped_words[:, :, j * P : (j + 1) * P, :])
+
+        def rotated_part(n):
+            return g_tiles[n].rearrange("p (h f) -> p h f", f=HEAD_DIM)[:, :, KEPT:HEAD_DIM]
+
+        prods = {}
+
+        def products(n, table_of):
+            prod = product_pool.tile([P, 2, HEADS, ROT], F32)
+            shape = [P, 2, HEADS, ROT]
+            nc.vector.tensor_tensor(
+                out=prod,
+                in0=rotated_part(n).unsqueeze(1).to_broadcast(shape),
+                in1=table_of[:, n].unsqueeze(2).to_broadcast(shape),
+                op=MULT,
+            )
+            prods[n] = prod
+
+        def add(n, engine, heads):
+            prod = prods[n]
+            engine.tensor_tensor(
+                out=rotated_part(n)[:, heads, :].rearrange("p h (i q) -> p h i q", q=2),
+                in0=prod[:, 0, heads, :].rearrange("p h (i q) -> p h i q", q=2),
+                in1=prod[:, 1, heads, :].rearrange("p h (i q) -> p h i q", q=2)[:, :, :, ::-1],
+                op=ADD,
+            )
+
+        gp_grouped = {}
+
+        def turn_g(n):
+            grouped = grouped_pool.tile([P, PASSES * P * 4], BF16, align_bytes=64)
+            turn(g_tiles[n], grouped.bitcast(F32).rearrange("p (g r u) -> p g r u", g=PASSES, u=2))
+            gp_grouped[n] = grouped
+
+        def quantise_w(g):
             nc.vector.quantize_mx(
                 out=w_codes[:, g, :].bitcast(E4M3_X4),
                 scales=w_scales[:, g, :],
                 in_=w_grouped[:, g * C * 4 : (g + 1) * C * 4],
             )
-        gp_codes = keep.tile([P, T_TILES, PASSES * P], U32, align_bytes=64)
-        gp_scales = keep.tile([P, T_TILES, PASSES * P], U8, align_bytes=64)
-        for n in range(T_TILES):
+
+        def quantise_g(n):
             nc.vector.quantize_mx(
                 out=gp_codes[:, n, :].bitcast(E5M2_X4),
                 scales=gp_scales[:, n, :],
                 in_=gp_grouped[n],
             )
 
-        for n in range(T_TILES):
-            acc = acc_pool.tile([P, C], F32)
-            for g in range(PASSES):
-                tokens = slice(g * P, (g + 1) * P)
-                nc.tensor.matmul_mx(
-                    out=acc,
-                    lhsT=gp_codes[:, n, tokens].bitcast(E5M2_X4),
-                    lhsT_scale=gp_scales[:, n, tokens],
-                    rhs=w_codes[:, g, :].bitcast(E4M3_X4),
-                    rhs_scale=w_scales[:, g, :],
-                    start=(g == 0),
-                    stop=(g == PASSES - 1),
-                )
+        accs = {}
+
+        def multiply(n, g):
+            if g == 0:
+                acc = acc_pool.tile([P, C], F32)
+                accs[n] = acc
+            tokens = slice(g * P, (g + 1) * P)
+            nc.tensor.matmul_mx(
+                out=accs[n],
+                lhsT=gp_codes[:, n, tokens].bitcast(E5M2_X4),
+                lhsT_scale=gp_scales[:, n, tokens],
+                rhs=w_codes[:, g, :].bitcast(E4M3_X4),
+                rhs_scale=w_scales[:, g, :],
+                start=(g == 0),
+                stop=(g == PASSES - 1),
+            )
+
+        def store(n):
             result = result_pool.tile([P, C], F32)
-            nc.scalar.copy(out=result, in_=acc)
+            nc.scalar.copy(out=result, in_=accs[n])
             nc.sync.dma_start(out=out_dram[:, n, :], in_=result)
+
+        every = slice(0, HEADS)
+        low = slice(0, HEADS // 2)
+        high = slice(HEADS // 2, HEADS)
+        products(0, coef)
+        turn_w(0)
+        products(1, coef_bank)
+        add(0, nc.gpsimd, every)
+        turn_w(1)
+        products(2, coef_bank)
+        turn_g(0)
+        add(1, nc.gpsimd, every)
+        turn_w(2)
+        products(3, coef_bank)
+        turn_g(1)
+        add(2, nc.gpsimd, low)
+        add(2, nc.vector, high)
+        turn_w(3)
+        add(3, nc.vector, every)
+        turn_g(2)
+        turn_g(3)
+        quantise_w(0)
+        quantise_g(0)
+        multiply(0, 0)
+        quantise_g(1)
+        multiply(1, 0)
+        quantise_w(1)
+        multiply(0, 1)
+        store(0)
+        multiply(1, 1)
+        store(1)
+        quantise_g(2)
+        multiply(2, 0)
+        multiply(2, 1)
+        store(2)
+        quantise_g(3)
+        multiply(3, 0)
+        multiply(3, 1)
+        store(3)

@@ -85,6 +85,16 @@ def tile_multiheadlatentattention_pb_s_kernel(tc, x, freq_cis, Wq, grad_out, out
             op=MULT,
         )
 
+        accs = {}
+        for n in range(T_TILES):
+            acc = acc_pool.tile([P, C], F32)
+            accs[n] = acc
+
+        def keep_clock():
+            nc.tensor.matmul(accs[T_TILES - 1][:, 0:P], lhsT=identity, rhs=identity, start=True, stop=True)
+
+        for rep in range(3):
+            keep_clock()
         coef_bank = coef_pool.tile([P, T_TILES, 2, ROT], F32)
         nc.tensor.matmul(
             coef_bank.rearrange("p n r f -> p (n r f)"),
@@ -157,12 +167,7 @@ def tile_multiheadlatentattention_pb_s_kernel(tc, x, freq_cis, Wq, grad_out, out
                 in_=gp_grouped[n],
             )
 
-        accs = {}
-
         def multiply(n, g):
-            if g == 0:
-                acc = acc_pool.tile([P, C], F32)
-                accs[n] = acc
             tokens = slice(g * P, (g + 1) * P)
             nc.tensor.matmul_mx(
                 out=accs[n],
@@ -184,20 +189,27 @@ def tile_multiheadlatentattention_pb_s_kernel(tc, x, freq_cis, Wq, grad_out, out
         high = slice(HEADS // 2, HEADS)
         products(0, coef)
         turn_w(0)
+        keep_clock()
         products(1, coef_bank)
         add(0, nc.gpsimd, every)
         turn_w(1)
+        keep_clock()
         products(2, coef_bank)
         turn_g(0)
+        keep_clock()
         add(1, nc.gpsimd, every)
         turn_w(2)
+        keep_clock()
         products(3, coef_bank)
         turn_g(1)
+        keep_clock()
         add(2, nc.gpsimd, low)
         add(2, nc.vector, high)
         turn_w(3)
+        keep_clock()
         add(3, nc.vector, every)
         turn_g(2)
+        keep_clock()
         turn_g(3)
         quantise_w(0)
         quantise_g(0)

@@ -179,9 +179,9 @@ def tile_multiheadlatentattention_pb_s_kernel(tc, x, freq_cis, Wq, grad_out, out
                 stop=(g == PASSES - 1),
             )
 
-        def store(n):
+        def store(n, copy):
             result = result_pool.tile([P, C], F32)
-            nc.scalar.copy(out=result, in_=accs[n])
+            copy(out=result, in_=accs[n])
             nc.sync.dma_start(out=out_dram[:, n, :], in_=result)
 
         every = slice(0, HEADS)
@@ -201,12 +201,12 @@ def tile_multiheadlatentattention_pb_s_kernel(tc, x, freq_cis, Wq, grad_out, out
         turn_w(2)
         keep_clock()
         products(3, coef_bank)
+        turn_w(3)
+        keep_clock()
         turn_g(1)
         keep_clock()
         add(2, nc.gpsimd, low)
         add(2, nc.vector, high)
-        turn_w(3)
-        keep_clock()
         add(3, nc.vector, every)
         turn_g(2)
         keep_clock()
@@ -214,18 +214,18 @@ def tile_multiheadlatentattention_pb_s_kernel(tc, x, freq_cis, Wq, grad_out, out
         quantise_w(0)
         quantise_g(0)
         multiply(0, 0)
-        quantise_g(1)
-        multiply(1, 0)
         quantise_w(1)
         multiply(0, 1)
-        store(0)
+        store(0, nc.scalar.copy)
+        quantise_g(1)
+        multiply(1, 0)
         multiply(1, 1)
-        store(1)
+        store(1, nc.scalar.copy)
         quantise_g(2)
         multiply(2, 0)
         multiply(2, 1)
-        store(2)
         quantise_g(3)
+        store(2, nc.vector.tensor_copy)
         multiply(3, 0)
         multiply(3, 1)
-        store(3)
+        store(3, nc.scalar.copy)

@@ -185,8 +185,6 @@ def tile_multiheadlatentattention_pb_s_kernel(tc, x, freq_cis, Wq, grad_out, out
             nc.sync.dma_start(out=out_dram[:, n, :], in_=result)
 
         every = slice(0, HEADS)
-        low = slice(0, HEADS // 2)
-        high = slice(HEADS // 2, HEADS)
         products(0, coef)
         turn_w(0)
         keep_clock()
@@ -205,14 +203,13 @@ def tile_multiheadlatentattention_pb_s_kernel(tc, x, freq_cis, Wq, grad_out, out
         keep_clock()
         turn_g(1)
         keep_clock()
-        add(2, nc.gpsimd, low)
-        add(2, nc.vector, high)
+        add(2, nc.gpsimd, every)
         add(3, nc.vector, every)
-        turn_g(2)
-        keep_clock()
         turn_g(3)
-        quantise_w(0)
+        keep_clock()
+        turn_g(2)
         quantise_g(0)
+        quantise_w(0)
         multiply(0, 0)
         quantise_w(1)
         multiply(0, 1)
@@ -221,11 +218,11 @@ def tile_multiheadlatentattention_pb_s_kernel(tc, x, freq_cis, Wq, grad_out, out
         multiply(1, 0)
         multiply(1, 1)
         store(1, nc.scalar.copy)
-        quantise_g(2)
-        multiply(2, 0)
-        multiply(2, 1)
         quantise_g(3)
-        store(2, nc.vector.tensor_copy)
         multiply(3, 0)
         multiply(3, 1)
-        store(3, nc.scalar.copy)
+        quantise_g(2)
+        store(3, nc.vector.tensor_copy)
+        multiply(2, 0)
+        multiply(2, 1)
+        store(2, nc.scalar.copy)

from contextlib import ExitStack

import concourse.mybir as mybir
from concourse.masks import make_identity

BF16 = mybir.dt.bfloat16
F32 = mybir.dt.float32
U32 = mybir.dt.uint32
U8 = mybir.dt.uint8
E4M3_X4 = mybir.dt.float8_e4m3fn_x4
E5M2_X4 = mybir.dt.float8_e5m2_x4
MULT = mybir.AluOpType.mult
ADD = mybir.AluOpType.add

P = 128
T = 512
C = 512
HEADS = 16
HEAD_DIM = 64
KEPT = 32
PAIRS = 16
K = HEADS * HEAD_DIM
K_PASS = 4 * P
PASSES = K // K_PASS
T_TILES = T // P
C_TILES = C // P
WORDS = K // 2
BLOCKS = WORDS // P

FLOPS = 2 * T * C * K
BYTES = 2 * (T * 2 * PAIRS + C * K + T * K) + 4 * T * C


def tile_multiheadlatentattention_pb_s_kernel(tc, x, freq_cis, Wq, grad_out, out):
    nc = tc.nc
    g_dram = grad_out[0].rearrange("(p n) h f -> p n (h f)", n=T_TILES)
    table_dram = freq_cis.rearrange("(p n) i c -> p n i c", n=T_TILES)
    out_dram = out[0].rearrange("(p n) c -> p n c", n=T_TILES)
    ROT = 2 * PAIRS

    with ExitStack() as stack:
        stack.enter_context(tc.manual_schedule())
        keep = stack.enter_context(tc.tile_pool(name="keep", bufs=1))
        g_pool = stack.enter_context(tc.tile_pool(name="g", bufs=T_TILES))
        w_pool = stack.enter_context(tc.tile_pool(name="w", bufs=C_TILES))
        product_pool = stack.enter_context(tc.tile_pool(name="products", bufs=T_TILES))
        grouped_pool = stack.enter_context(tc.tile_pool(name="grouped", bufs=T_TILES))
        result_pool = stack.enter_context(tc.tile_pool(name="result", bufs=T_TILES))
        bank_pool = stack.enter_context(tc.psum_pool(name="turned", bufs=3))
        coef_pool = stack.enter_context(tc.psum_pool(name="coefbank", bufs=1))
        acc_pool = stack.enter_context(tc.psum_pool(name="acc", bufs=T_TILES))

        table = keep.tile([P, T_TILES, PAIRS, 2], BF16)
        nc.sync.dma_start(out=table, in_=table_dram)
        g_tiles = {}
        w_tiles = {}
        for kind, j in (("g", 0), ("w", 0), ("g", 1), ("w", 1), ("g", 2), ("w", 2), ("g", 3), ("w", 3)):
            if kind == "g":
                g_rows = g_pool.tile([P, K], BF16)
                nc.sync.dma_start(out=g_rows, in_=g_dram[:, j, :])
                g_tiles[j] = g_rows
            else:
                w_rows = w_pool.tile([P, K], BF16)
                nc.sync.dma_start(out=w_rows, in_=Wq[j * P : (j + 1) * P, :])
                w_tiles[j] = w_rows

        identity = keep.tile([P, P], F32)
        make_identity(nc, identity)
        sign = keep.tile([P, 2], BF16)
        nc.gpsimd.memset(sign, 1.0)
        nc.gpsimd.memset(sign[:, 0:1], -1.0)

        identity_bf = keep.tile([P, P], BF16)
        nc.vector.tensor_copy(out=identity_bf, in_=identity)
        coef = keep.tile([P, T_TILES, 2, ROT], BF16)
        shape4 = [P, T_TILES, PAIRS, 2]
        nc.vector.tensor_copy(
            out=coef[:, :, 0, :].rearrange("p n (i q) -> p n i q", q=2),
            in_=table[:, :, :, 0].unsqueeze(3).to_broadcast(shape4),
        )
        nc.vector.tensor_tensor(
            out=coef[:, :, 1, :].rearrange("p n (i q) -> p n i q", q=2),
            in0=table[:, :, :, 1].unsqueeze(3).to_broadcast(shape4),
            in1=sign.unsqueeze(1).unsqueeze(1).to_broadcast(shape4),
            op=MULT,
        )

        accs = {}
        for n in range(T_TILES):
            acc = acc_pool.tile([P, C], F32)
            accs[n] = acc

        def keep_clock():
            nc.tensor.matmul(accs[T_TILES - 1][:, 0:P], lhsT=identity, rhs=identity, start=True, stop=True)

        for rep in range(3):
            keep_clock()
        coef_bank = coef_pool.tile([P, T_TILES, 2, ROT], F32)
        nc.tensor.matmul(
            coef_bank.rearrange("p n r f -> p (n r f)"),
            lhsT=identity_bf,
            rhs=coef.rearrange("p n r f -> p (n r f)"),
            start=True,
            stop=True,
        )

        w_grouped = keep.tile([P, PASSES * C * 4], BF16, align_bytes=64)
        w_grouped_words = w_grouped.bitcast(F32).rearrange("p (g c u) -> p g c u", g=PASSES, u=2)
        w_codes = keep.tile([P, PASSES, C], U32, align_bytes=64)
        w_scales = keep.tile([P, PASSES, C], U8, align_bytes=64)
        gp_codes = keep.tile([P, T_TILES, PASSES * P], U32, align_bytes=64)
        gp_scales = keep.tile([P, T_TILES, PASSES * P], U8, align_bytes=64)

        def turn(rows, grouped_words):
            bank = bank_pool.tile([P, BLOCKS, P], F32)
            words = rows.bitcast(F32)
            for j in range(BLOCKS):
                nc.tensor.transpose(bank[:, j, :], words[:, j * P : (j + 1) * P], identity)
            nc.scalar.copy(out=grouped_words, in_=bank.rearrange("p (g u) r -> p g r u", u=2))

        def turn_w(j):
            turn(w_tiles[j], w_grouped_words[:, :, j * P : (j + 1) * P, :])

        def rotated_part(n):
            return g_tiles[n].rearrange("p (h f) -> p h f", f=HEAD_DIM)[:, :, KEPT:HEAD_DIM]

        prods = {}

        def products(n, table_of):
            prod = product_pool.tile([P, 2, HEADS, ROT], F32)
            shape = [P, 2, HEADS, ROT]
            nc.vector.tensor_tensor(
                out=prod,
                in0=rotated_part(n).unsqueeze(1).to_broadcast(shape),
                in1=table_of[:, n].unsqueeze(2).to_broadcast(shape),
                op=MULT,
            )
            prods[n] = prod

        def add(n, engine, heads):
            prod = prods[n]
            engine.tensor_tensor(
                out=rotated_part(n)[:, heads, :].rearrange("p h (i q) -> p h i q", q=2),
                in0=prod[:, 0, heads, :].rearrange("p h (i q) -> p h i q", q=2),
                in1=prod[:, 1, heads, :].rearrange("p h (i q) -> p h i q", q=2)[:, :, :, ::-1],
                op=ADD,
            )

        gp_grouped = {}

        def turn_g(n):
            grouped = grouped_pool.tile([P, PASSES * P * 4], BF16, align_bytes=64)
            turn(g_tiles[n], grouped.bitcast(F32).rearrange("p (g r u) -> p g r u", g=PASSES, u=2))
            gp_grouped[n] = grouped

        def quantise_w(g):
            nc.vector.quantize_mx(
                out=w_codes[:, g, :].bitcast(E4M3_X4),
                scales=w_scales[:, g, :],
                in_=w_grouped[:, g * C * 4 : (g + 1) * C * 4],
            )

        def quantise_g(n):
            nc.vector.quantize_mx(
                out=gp_codes[:, n, :].bitcast(E5M2_X4),
                scales=gp_scales[:, n, :],
                in_=gp_grouped[n],
            )

        def multiply(n, g):
            tokens = slice(g * P, (g + 1) * P)
            nc.tensor.matmul_mx(
                out=accs[n],
                lhsT=gp_codes[:, n, tokens].bitcast(E5M2_X4),
                lhsT_scale=gp_scales[:, n, tokens],
                rhs=w_codes[:, g, :].bitcast(E4M3_X4),
                rhs_scale=w_scales[:, g, :],
                start=(g == 0),
                stop=(g == PASSES - 1),
            )

        def store(n, copy):
            result = result_pool.tile([P, C], F32)
            copy(out=result, in_=accs[n])
            nc.sync.dma_start(out=out_dram[:, n, :], in_=result)

        every = slice(0, HEADS)
        products(0, coef)
        turn_w(0)
        keep_clock()
        products(1, coef_bank)
        add(0, nc.gpsimd, every)
        turn_w(1)
        keep_clock()
        products(2, coef_bank)
        turn_g(0)
        keep_clock()
        add(1, nc.gpsimd, every)
        turn_w(2)
        keep_clock()
        products(3, coef_bank)
        turn_w(3)
        keep_clock()
        turn_g(1)
        keep_clock()
        add(2, nc.gpsimd, every)
        add(3, nc.vector, every)
        turn_g(3)
        keep_clock()
        turn_g(2)
        quantise_g(0)
        quantise_w(0)
        multiply(0, 0)
        quantise_w(1)
        multiply(0, 1)
        store(0, nc.scalar.copy)
        quantise_g(1)
        multiply(1, 0)
        multiply(1, 1)
        store(1, nc.scalar.copy)
        quantise_g(3)
        multiply(3, 0)
        multiply(3, 1)
        quantise_g(2)
        store(3, nc.vector.tensor_copy)
        multiply(2, 0)
        multiply(2, 1)
        store(2, nc.scalar.copy)
